import numpy as np
import ml_dtypes


def mxq(x, axis, fmt="e4m3"):
    dtype, down = {"e4m3": (ml_dtypes.float8_e4m3fn, 7), "e5m2": (ml_dtypes.float8_e5m2, 14)}[fmt]
    v = np.moveaxis(np.asarray(x, np.float32).astype(ml_dtypes.bfloat16).astype(np.float64), axis, -1)
    blocks = v.reshape(v.shape[:-1] + (-1, 32))
    amax = np.abs(blocks).max(-1, keepdims=True)
    byte = np.maximum(np.where(amax > 0, np.frexp(amax)[1] - 1 + 127, 0) - down, 1)
    scale = np.exp2(byte - 127.0)
    codes = (blocks / scale).astype(np.float32).astype(dtype).astype(np.float64)
    return np.moveaxis((codes * scale).reshape(v.shape), -1, axis)


WIDE = False


def mx_kscale(k):
    if not WIDE:
        return np.ones(k)
    levels = np.array([10, -10, 5, -5, 0])
    a = np.random.permutation(np.resize(levels, k // 512 * 4)).reshape(k // 512, 4)
    idx = np.arange(k)
    return np.exp2(a[idx // 512, idx % 128 // 32])


BF16 = ml_dtypes.bfloat16


def bf(x):
    return np.asarray(x, np.float32).astype(BF16)


def f64(x):
    return np.asarray(x).astype(np.float64)


BS, DC, R, C = 1, 128, 64, 64
N = R * C
THRESH = 0.85


def setup_inputs():
    s = mx_kscale(N)
    u = s / s.min()
    g = 2.0 ** np.round(np.log2(u.mean()))
    seg = np.random.standard_normal((BS, DC, R, C)) * 0.1 * np.sqrt(N)
    W0 = f64(bf(np.random.random_sample((BS, N, N))))
    return {"seg": bf(seg * (g / u).reshape(1, 1, R, C)),
            "W": bf(np.where(W0 > THRESH, W0 * u, W0))}


def reference(seg, W):
    seg, W = f64(seg), f64(W)
    bs, d, r, c = seg.shape
    Wt = np.where(W > THRESH, W, 0.0)
    D = Wt / Wt.sum(axis=-1, keepdims=True)
    seg_flat = seg.reshape(bs, d, r * c)
    out = mxq(seg_flat, 2, "e4m3") @ mxq(D, 2, "e4m3").transpose(0, 2, 1)
    return out.reshape(bs, d, r, c)

@@ -1,0 +1,157 @@
+from contextlib import ExitStack
+
+import concourse.bass as bass
+import concourse.mybir as mybir
+import concourse.tile as tile
+from concourse.masks import make_identity
+
+BF16 = mybir.dt.bfloat16
+F32 = mybir.dt.float32
+U32 = mybir.dt.uint32
+U8 = mybir.dt.uint8
+FP8X4 = mybir.dt.float8_e4m3fn_x4
+ALU = mybir.AluOpType
+ACT = mybir.ActivationFunctionType
+
+P = 128
+N = 4096
+THRESH = 0.85
+ROWS = 64
+TILES = N // ROWS
+GROUP = 8
+PASSES = 8
+FLOPS = 2 * 128 * N * N
+
+B_ON_VECTOR = (3,)
+
+
+def tile_regu_diff_kernel(tc, seg, W, out):
+    nc = tc.nc
+    seg_flat = seg.rearrange("b d r c -> (b d) (r c)")
+    out_flat = out.rearrange("b d r c -> (b d) (r c)")
+    w2 = W.rearrange("b m n -> (b m) n")
+
+    with ExitStack() as ctx:
+        const = ctx.enter_context(tc.tile_pool(name="const", bufs=1))
+        win_pool = ctx.enter_context(tc.tile_pool(name="win", bufs=6))
+        wt_pool = ctx.enter_context(tc.tile_pool(name="wt", bufs=4))
+        d_pool = ctx.enter_context(tc.tile_pool(name="d", bufs=4))
+        g_pool = ctx.enter_context(tc.tile_pool(name="grouped", bufs=2))
+        q_pool = ctx.enter_context(tc.tile_pool(name="quant", bufs=2))
+        res_pool = ctx.enter_context(tc.tile_pool(name="res", bufs=2))
+        psum_t = ctx.enter_context(tc.psum_pool(name="psum_t", bufs=4))
+        psum_s = ctx.enter_context(tc.psum_pool(name="psum_s", bufs=2))
+        psum_a = ctx.enter_context(tc.psum_pool(name="psum_a", bufs=2))
+
+        ident = const.tile([P, P], BF16, name="ident")
+        make_identity(nc, ident[:])
+        ident32 = const.tile([P, P], F32, name="ident32")
+        make_identity(nc, ident32[:])
+        pair = const.tile([P, P], F32, name="pair")
+        i3 = ident32[:].rearrange("p (j e) -> p j e", e=2)
+        p3 = pair[:].rearrange("p (j e) -> p j e", e=2)
+        for e in range(2):
+            nc.vector.tensor_tensor(out=p3[:, :, e], in0=i3[:, :, 0], in1=i3[:, :, 1], op=ALU.add)
+
+        part = const.tile([P, TILES], F32, name="part")
+        recip = const.tile([P, TILES], F32, name="recip")
+
+        seg_sb = const.tile([P, N], BF16, name="seg_sb")
+        seg_g = const.tile([P, PASSES, P, 4], BF16, name="seg_g", align_bytes=64)
+        seg_codes = const.tile([P, PASSES * P], U32, name="seg_codes", align_bytes=64)
+        seg_scales = const.tile([P, PASSES * P], U8, name="seg_scales", align_bytes=64)
+
+        def prepare_seg():
+            nc.sync.dma_start(out=seg_sb[:], in_=seg_flat)
+            for half in range(PASSES // 2):
+                xs = psum_t.tile([P, 1024], BF16, tag="xt", name="xs")
+                xsv = xs[:].rearrange("p (a s d) -> p a s d", a=2, s=4)
+                for a in range(2):
+                    g = 2 * half + a
+                    for u in range(2):
+                        for e in range(2):
+                            k0 = 512 * g + 256 * e + 128 * u
+                            nc.tensor.transpose(xsv[:, a, 2 * u + e, :], seg_sb[:, k0 : k0 + P], ident[:])
+                nc.scalar.copy(
+                    out=seg_g[:, 2 * half : 2 * half + 2, :, :],
+                    in_=xs[:].rearrange("p (a s d) -> p a d s", a=2, s=4),
+                )
+            nc.vector.quantize_mx(
+                out=seg_codes[:].bitcast(FP8X4),
+                scales=seg_scales[:],
+                in_=seg_g[:].rearrange("p g d s -> p (g d s)"),
+            )
+
+        grouped = None
+        for i in range(TILES):
+            il = i % GROUP
+            r0 = i * ROWS
+            win = win_pool.tile([P, 2048], BF16, name="win")
+            src = w2[r0 : r0 + ROWS, :].rearrange("m (g e x) -> e m g x", e=2, x=256)
+            for e in range(2):
+                nc.sync.dma_start(
+                    out=win[e:P:2, :].rearrange("q (g x) -> q g x", x=256),
+                    in_=src[e, :, :, :],
+                )
+            if i == 1:
+                prepare_seg()
+
+            wt = wt_pool.tile([P, 2048], BF16, name="wt")
+            nc.vector.scalar_tensor_tensor(
+                out=wt[:],
+                in0=win[:],
+                scalar=THRESH,
+                in1=win[:],
+                op0=ALU.is_gt,
+                op1=ALU.mult,
+                accum_out=part[:, i : i + 1],
+            )
+            sums = psum_s.tile([P, 1], F32, name="sums")
+            nc.tensor.matmul(out=sums[:], lhsT=pair[:], rhs=part[:, i : i + 1], start=True, stop=True)
+            nc.vector.reciprocal(out=recip[:, i : i + 1], in_=sums[:])
+
+            d = d_pool.tile([P, 2048], BF16, name="d")
+            if il in B_ON_VECTOR:
+                nc.vector.tensor_scalar(
+                    out=d[:], in0=wt[:], scalar1=recip[:, i : i + 1], scalar2=None, op0=ALU.mult
+                )
+            else:
+                nc.scalar.activation(out=d[:], in_=wt[:], func=ACT.Copy, scale=recip[:, i : i + 1])
+
+            if il == 0:
+                grouped = g_pool.tile([P, PASSES, 4 * ROWS * GROUP], BF16, name="grouped", align_bytes=64)
+            for h in range(2):
+                xt = psum_t.tile([P, 1024], BF16, tag="xt", name="xt")
+                xv = xt[:].rearrange("p (g m u e) -> p g u m e", g=4, m=ROWS, u=2, e=2)
+                for gl in range(4):
+                    g = 4 * h + gl
+                    for u in range(2):
+                        c0 = 256 * g + 128 * u
+                        nc.tensor.transpose(xv[:, gl, u, :, :], d[:, c0 : c0 + P], ident[:])
+                nc.scalar.copy(
+                    out=grouped[:, 4 * h : 4 * h + 4, 256 * il : 256 * (il + 1)],
+                    in_=xt[:].rearrange("p (g c) -> p g c", g=4),
+                )
+
+            if il == GROUP - 1:
+                codes = q_pool.tile([P, PASSES, 512], U32, name="codes", align_bytes=64)
+                scales = q_pool.tile([P, PASSES, 512], U8, name="scales", align_bytes=64)
+                for g in range(PASSES):
+                    nc.vector.quantize_mx(
+                        out=codes[:, g, :].bitcast(FP8X4), scales=scales[:, g, :], in_=grouped[:, g, :]
+                    )
+                acc = psum_a.tile([P, 512], F32, name="acc")
+                for g in range(PASSES):
+                    nc.tensor.matmul_mx(
+                        out=acc[:],
+                        lhsT=seg_codes[:, g * P : (g + 1) * P].bitcast(FP8X4),
+                        lhsT_scale=seg_scales[:, g * P : (g + 1) * P],
+                        rhs=codes[:, g, :].bitcast(FP8X4),
+                        rhs_scale=scales[:, g, :],
+                        start=(g == 0),
+                        stop=(g == PASSES - 1),
+                    )
+                res = res_pool.tile([P, 512], F32, name="res")
+                nc.vector.tensor_copy(out=res[:], in_=acc[:])
+                m0 = (i // GROUP) * 512
+                nc.sync.dma_start(out=out_flat[:, m0 : m0 + 512], in_=res[:])

@@ -22,7 +22,7 @@ GROUP = 8
 PASSES = 8
 FLOPS = 2 * 128 * N * N
 
-B_ON_VECTOR = (3,)
+B_ON_VECTOR = (1, 4, 6)
 
 
 def tile_regu_diff_kernel(tc, seg, W, out):

@@ -1,8 +1,6 @@
 from contextlib import ExitStack
 
-import concourse.bass as bass
 import concourse.mybir as mybir
-import concourse.tile as tile
 from concourse.masks import make_identity
 
 BF16 = mybir.dt.bfloat16
@@ -17,12 +15,18 @@ P = 128
 N = 4096
 THRESH = 0.85
 ROWS = 64
+HALF = N // 2
 TILES = N // ROWS
-GROUP = 8
+DUOS = TILES // 2
 PASSES = 8
 FLOPS = 2 * 128 * N * N
 
-B_ON_VECTOR = (1, 4, 6)
+AHEAD = 3
+LAG_SCALE = 1
+LAG_TURN = 2
+LAG_QUANT = 4
+LAG_MX = 5
+V_COLS = HALF
 
 
 def tile_regu_diff_kernel(tc, seg, W, out):
@@ -32,15 +36,16 @@ def tile_regu_diff_kernel(tc, seg, W, out):
     w2 = W.rearrange("b m n -> (b m) n")
 
     with ExitStack() as ctx:
+        ctx.enter_context(tc.manual_schedule())
         const = ctx.enter_context(tc.tile_pool(name="const", bufs=1))
-        win_pool = ctx.enter_context(tc.tile_pool(name="win", bufs=6))
-        wt_pool = ctx.enter_context(tc.tile_pool(name="wt", bufs=4))
-        d_pool = ctx.enter_context(tc.tile_pool(name="d", bufs=4))
-        g_pool = ctx.enter_context(tc.tile_pool(name="grouped", bufs=2))
-        q_pool = ctx.enter_context(tc.tile_pool(name="quant", bufs=2))
+        win_pool = ctx.enter_context(tc.tile_pool(name="win", bufs=2 * AHEAD + 2))
+        wt_pool = ctx.enter_context(tc.tile_pool(name="wt", bufs=6))
+        d_pool = ctx.enter_context(tc.tile_pool(name="d", bufs=6))
+        g_pool = ctx.enter_context(tc.tile_pool(name="grouped", bufs=4))
+        q_pool = ctx.enter_context(tc.tile_pool(name="quant", bufs=3))
         res_pool = ctx.enter_context(tc.tile_pool(name="res", bufs=2))
-        psum_t = ctx.enter_context(tc.psum_pool(name="psum_t", bufs=4))
-        psum_s = ctx.enter_context(tc.psum_pool(name="psum_s", bufs=2))
+        psum_t = ctx.enter_context(tc.psum_pool(name="psum_t", bufs=5))
+        psum_s = ctx.enter_context(tc.psum_pool(name="psum_s", bufs=1))
         psum_a = ctx.enter_context(tc.psum_pool(name="psum_a", bufs=2))
 
         ident = const.tile([P, P], BF16, name="ident")
@@ -55,103 +60,155 @@ def tile_regu_diff_kernel(tc, seg, W, out):
 
         part = const.tile([P, TILES], F32, name="part")
         recip = const.tile([P, TILES], F32, name="recip")
-
         seg_sb = const.tile([P, N], BF16, name="seg_sb")
         seg_g = const.tile([P, PASSES, P, 4], BF16, name="seg_g", align_bytes=64)
         seg_codes = const.tile([P, PASSES * P], U32, name="seg_codes", align_bytes=64)
         seg_scales = const.tile([P, PASSES * P], U8, name="seg_scales", align_bytes=64)
 
-        def prepare_seg():
-            nc.sync.dma_start(out=seg_sb[:], in_=seg_flat)
-            for half in range(PASSES // 2):
-                xs = psum_t.tile([P, 1024], BF16, tag="xt", name="xs")
-                xsv = xs[:].rearrange("p (a s d) -> p a s d", a=2, s=4)
-                for a in range(2):
-                    g = 2 * half + a
-                    for u in range(2):
-                        for e in range(2):
-                            k0 = 512 * g + 256 * e + 128 * u
-                            nc.tensor.transpose(xsv[:, a, 2 * u + e, :], seg_sb[:, k0 : k0 + P], ident[:])
-                nc.scalar.copy(
-                    out=seg_g[:, 2 * half : 2 * half + 2, :, :],
-                    in_=xs[:].rearrange("p (a s d) -> p a d s", a=2, s=4),
-                )
-            nc.vector.quantize_mx(
-                out=seg_codes[:].bitcast(FP8X4),
-                scales=seg_scales[:],
-                in_=seg_g[:].rearrange("p g d s -> p (g d s)"),
-            )
+        wins = {}
+        wts = {}
+        ds = {}
+        groupeds = {}
+        quants = {}
+        accs = {}
 
-        grouped = None
-        for i in range(TILES):
-            il = i % GROUP
-            r0 = i * ROWS
-            win = win_pool.tile([P, 2048], BF16, name="win")
-            src = w2[r0 : r0 + ROWS, :].rearrange("m (g e x) -> e m g x", e=2, x=256)
+        def load(t):
+            win = win_pool.tile([P, HALF], BF16, name="win")
+            src = w2[t * ROWS : (t + 1) * ROWS, :].rearrange("m (g e x) -> e m g x", e=2, x=256)
             for e in range(2):
                 nc.sync.dma_start(
-                    out=win[e:P:2, :].rearrange("q (g x) -> q g x", x=256),
-                    in_=src[e, :, :, :],
+                    out=win[e:P:2, :].rearrange("q (g x) -> q g x", x=256), in_=src[e, :, :, :]
                 )
-            if i == 1:
-                prepare_seg()
+            wins[t] = win
 
-            wt = wt_pool.tile([P, 2048], BF16, name="wt")
+        def threshold(t):
+            wt = wt_pool.tile([P, HALF], BF16, name="wt")
             nc.vector.scalar_tensor_tensor(
                 out=wt[:],
-                in0=win[:],
+                in0=wins[t][:],
                 scalar=THRESH,
-                in1=win[:],
+                in1=wins[t][:],
                 op0=ALU.is_gt,
                 op1=ALU.mult,
-                accum_out=part[:, i : i + 1],
+                accum_out=part[:, t : t + 1],
             )
-            sums = psum_s.tile([P, 1], F32, name="sums")
-            nc.tensor.matmul(out=sums[:], lhsT=pair[:], rhs=part[:, i : i + 1], start=True, stop=True)
-            nc.vector.reciprocal(out=recip[:, i : i + 1], in_=sums[:])
+            wts[t] = wt
 
-            d = d_pool.tile([P, 2048], BF16, name="d")
-            if il in B_ON_VECTOR:
-                nc.vector.tensor_scalar(
-                    out=d[:], in0=wt[:], scalar1=recip[:, i : i + 1], scalar2=None, op0=ALU.mult
+        sums_of = {}
+
+        def pair_sums(s):
+            sums = psum_s.tile([P, 2], F32, name="sums")
+            nc.tensor.matmul(out=sums[:], lhsT=pair[:], rhs=part[:, 2 * s : 2 * s + 2], start=True, stop=True)
+            sums_of[s] = sums
+
+        def reciprocal(s):
+            nc.vector.reciprocal(out=recip[:, 2 * s : 2 * s + 2], in_=sums_of[s][:])
+
+        def scale(s):
+            a = 2 * s
+            b = 2 * s + 1
+            da = d_pool.tile([P, HALF], BF16, name="d")
+            db = d_pool.tile([P, HALF], BF16, name="d")
+            ds[a] = da
+            ds[b] = db
+            cut = HALF - V_COLS
+            nc.vector.tensor_scalar(
+                out=db[:, cut:], in0=wts[b][:, cut:], scalar1=recip[:, b : b + 1], scalar2=None, op0=ALU.mult
+            )
+            nc.scalar.activation(out=da[:], in_=wts[a][:], func=ACT.Copy, scale=recip[:, a : a + 1])
+            if cut > 0:
+                nc.scalar.activation(
+                    out=db[:, :cut], in_=wts[b][:, :cut], func=ACT.Copy, scale=recip[:, b : b + 1]
                 )
-            else:
-                nc.scalar.activation(out=d[:], in_=wt[:], func=ACT.Copy, scale=recip[:, i : i + 1])
 
-            if il == 0:
-                grouped = g_pool.tile([P, PASSES, 4 * ROWS * GROUP], BF16, name="grouped", align_bytes=64)
-            for h in range(2):
+        def turn(s):
+            grouped = g_pool.tile([P, PASSES * 512], BF16, name="grouped", align_bytes=64)
+            groupeds[s] = grouped
+            banks = []
+            for bank in range(4):
                 xt = psum_t.tile([P, 1024], BF16, tag="xt", name="xt")
-                xv = xt[:].rearrange("p (g m u e) -> p g u m e", g=4, m=ROWS, u=2, e=2)
-                for gl in range(4):
-                    g = 4 * h + gl
-                    for u in range(2):
-                        c0 = 256 * g + 128 * u
-                        nc.tensor.transpose(xv[:, gl, u, :, :], d[:, c0 : c0 + P], ident[:])
-                nc.scalar.copy(
-                    out=grouped[:, 4 * h : 4 * h + 4, 256 * il : 256 * (il + 1)],
-                    in_=xt[:].rearrange("p (g c) -> p g c", g=4),
+                xv = xt[:].rearrange("p (g j m u e) -> p g j u m e", g=2, j=2, m=ROWS, u=2, e=2)
+                for gl in range(2):
+                    g = 2 * bank + gl
+                    for j in range(2):
+                        for u in range(2):
+                            c0 = 256 * g + 128 * u
+                            nc.tensor.transpose(xv[:, gl, j, u, :, :], ds[2 * s + j][:, c0 : c0 + P], ident[:])
+                banks.append(xt)
+            for bank in range(4):
+                nc.scalar.copy(out=grouped[:, 1024 * bank : 1024 * (bank + 1)], in_=banks[bank][:])
+
+        def quantise(s):
+            codes = q_pool.tile([P, PASSES * P], U32, name="codes", align_bytes=64)
+            scales = q_pool.tile([P, PASSES * P], U8, name="scales", align_bytes=64)
+            nc.vector.quantize_mx(out=codes[:].bitcast(FP8X4), scales=scales[:], in_=groupeds[s][:])
+            quants[s] = (codes, scales)
+
+        def multiply(s):
+            if s % 4 == 0:
+                accs[s // 4] = psum_a.tile([P, 512], F32, name="acc")
+            acc = accs[s // 4]
+            codes, scales = quants[s]
+            c0 = (s % 4) * P
+            for g in range(PASSES):
+                cols = slice(g * P, (g + 1) * P)
+                nc.tensor.matmul_mx(
+                    out=acc[:, c0 : c0 + P],
+                    lhsT=seg_codes[:, cols].bitcast(FP8X4),
+                    lhsT_scale=seg_scales[:, cols],
+                    rhs=codes[:, cols].bitcast(FP8X4),
+                    rhs_scale=scales[:, cols],
+                    start=(g == 0),
+                    stop=(g == PASSES - 1),
                 )
 
-            if il == GROUP - 1:
-                codes = q_pool.tile([P, PASSES, 512], U32, name="codes", align_bytes=64)
-                scales = q_pool.tile([P, PASSES, 512], U8, name="scales", align_bytes=64)
-                for g in range(PASSES):
-                    nc.vector.quantize_mx(
-                        out=codes[:, g, :].bitcast(FP8X4), scales=scales[:, g, :], in_=grouped[:, g, :]
-                    )
-                acc = psum_a.tile([P, 512], F32, name="acc")
-                for g in range(PASSES):
-                    nc.tensor.matmul_mx(
-                        out=acc[:],
-                        lhsT=seg_codes[:, g * P : (g + 1) * P].bitcast(FP8X4),
-                        lhsT_scale=seg_scales[:, g * P : (g + 1) * P],
-                        rhs=codes[:, g, :].bitcast(FP8X4),
-                        rhs_scale=scales[:, g, :],
-                        start=(g == 0),
-                        stop=(g == PASSES - 1),
-                    )
-                res = res_pool.tile([P, 512], F32, name="res")
-                nc.vector.tensor_copy(out=res[:], in_=acc[:])
-                m0 = (i // GROUP) * 512
-                nc.sync.dma_start(out=out_flat[:, m0 : m0 + 512], in_=res[:])
+        def store(q):
+            res = res_pool.tile([P, 512], F32, name="res")
+            nc.vector.tensor_copy(out=res[:], in_=accs[q][:])
+            nc.sync.dma_start(out=out_flat[:, 512 * q : 512 * (q + 1)], in_=res[:])
+
+        for t in range(4):
+            load(t)
+        nc.sync.dma_start(out=seg_sb[:], in_=seg_flat)
+        for t in range(4, 2 * AHEAD):
+            load(t)
+        for half in range(PASSES // 2):
+            xs = psum_t.tile([P, 1024], BF16, tag="xt", name="xs")
+            xsv = xs[:].rearrange("p (a s d) -> p a s d", a=2, s=4)
+            for a in range(2):
+                g = 2 * half + a
+                for u in range(2):
+                    for e in range(2):
+                        k0 = 512 * g + 256 * e + 128 * u
+                        nc.tensor.transpose(xsv[:, a, 2 * u + e, :], seg_sb[:, k0 : k0 + P], ident[:])
+            nc.scalar.copy(
+                out=seg_g[:, 2 * half : 2 * half + 2, :, :],
+                in_=xs[:].rearrange("p (a s d) -> p a d s", a=2, s=4),
+            )
+
+        for s in range(DUOS + LAG_MX + 1):
+            if s + AHEAD < DUOS:
+                load(2 * (s + AHEAD))
+                load(2 * (s + AHEAD) + 1)
+            if s < DUOS:
+                threshold(2 * s)
+            if 0 <= s - LAG_SCALE < DUOS:
+                reciprocal(s - LAG_SCALE)
+                scale(s - LAG_SCALE)
+            if s == 2:
+                nc.vector.quantize_mx(
+                    out=seg_codes[:].bitcast(FP8X4),
+                    scales=seg_scales[:],
+                    in_=seg_g[:].rearrange("p g d s -> p (g d s)"),
+                )
+            if 0 <= s - LAG_MX < DUOS:
+                multiply(s - LAG_MX)
+            if 0 <= s - LAG_TURN < DUOS:
+                turn(s - LAG_TURN)
+            if 0 <= s - LAG_QUANT < DUOS:
+                quantise(s - LAG_QUANT)
+            if s < DUOS:
+                threshold(2 * s + 1)
+                pair_sums(s)
+            if 0 <= s - LAG_MX < DUOS and (s - LAG_MX) % 4 == 3:
+                store((s - LAG_MX) // 4)

@@ -26,7 +26,7 @@ LAG_SCALE = 1
 LAG_TURN = 2
 LAG_QUANT = 4
 LAG_MX = 5
-V_COLS = HALF
+V_COLS = 768
 
 
 def tile_regu_diff_kernel(tc, seg, W, out):
@@ -104,22 +104,31 @@ def tile_regu_diff_kernel(tc, seg, W, out):
         def reciprocal(s):
             nc.vector.reciprocal(out=recip[:, 2 * s : 2 * s + 2], in_=sums_of[s][:])
 
-        def scale(s):
+        def scale_scalar(s):
             a = 2 * s
             b = 2 * s + 1
-            da = d_pool.tile([P, HALF], BF16, name="d")
-            db = d_pool.tile([P, HALF], BF16, name="d")
-            ds[a] = da
-            ds[b] = db
+            ds[a] = d_pool.tile([P, HALF], BF16, name="d")
+            ds[b] = d_pool.tile([P, HALF], BF16, name="d")
+            if s == DUOS - 1:
+                return
             cut = HALF - V_COLS
-            nc.vector.tensor_scalar(
-                out=db[:, cut:], in0=wts[b][:, cut:], scalar1=recip[:, b : b + 1], scalar2=None, op0=ALU.mult
+            nc.scalar.activation(out=ds[a][:], in_=wts[a][:], func=ACT.Copy, scale=recip[:, a : a + 1])
+            nc.scalar.activation(
+                out=ds[b][:, :cut], in_=wts[b][:, :cut], func=ACT.Copy, scale=recip[:, b : b + 1]
             )
-            nc.scalar.activation(out=da[:], in_=wts[a][:], func=ACT.Copy, scale=recip[:, a : a + 1])
-            if cut > 0:
-                nc.scalar.activation(
-                    out=db[:, :cut], in_=wts[b][:, :cut], func=ACT.Copy, scale=recip[:, b : b + 1]
+
+        def scale_vector(s):
+            a = 2 * s
+            b = 2 * s + 1
+            cut = HALF - V_COLS
+            if s == DUOS - 1:
+                cut = 0
+                nc.vector.tensor_scalar(
+                    out=ds[a][:], in0=wts[a][:], scalar1=recip[:, a : a + 1], scalar2=None, op0=ALU.mult
                 )
+            nc.vector.tensor_scalar(
+                out=ds[b][:, cut:], in0=wts[b][:, cut:], scalar1=recip[:, b : b + 1], scalar2=None, op0=ALU.mult
+            )
 
         def turn(s):
             grouped = g_pool.tile([P, PASSES * 512], BF16, name="grouped", align_bytes=64)
@@ -141,7 +150,14 @@ def tile_regu_diff_kernel(tc, seg, W, out):
         def quantise(s):
             codes = q_pool.tile([P, PASSES * P], U32, name="codes", align_bytes=64)
             scales = q_pool.tile([P, PASSES * P], U8, name="scales", align_bytes=64)
-            nc.vector.quantize_mx(out=codes[:].bitcast(FP8X4), scales=scales[:], in_=groupeds[s][:])
+            pieces = 4 if s == DUOS - 1 else 1
+            words = PASSES * P // pieces
+            for i in range(pieces):
+                nc.vector.quantize_mx(
+                    out=codes[:, i * words : (i + 1) * words].bitcast(FP8X4),
+                    scales=scales[:, i * words : (i + 1) * words],
+                    in_=groupeds[s][:, 4 * i * words : 4 * (i + 1) * words],
+                )
             quants[s] = (codes, scales)
 
         def multiply(s):
@@ -162,10 +178,10 @@ def tile_regu_diff_kernel(tc, seg, W, out):
                     stop=(g == PASSES - 1),
                 )
 
-        def store(q):
+        def store(q, c0, c1):
             res = res_pool.tile([P, 512], F32, name="res")
-            nc.vector.tensor_copy(out=res[:], in_=accs[q][:])
-            nc.sync.dma_start(out=out_flat[:, 512 * q : 512 * (q + 1)], in_=res[:])
+            nc.scalar.copy(out=res[:, c0:c1], in_=accs[q][:, c0:c1])
+            nc.sync.dma_start(out=out_flat[:, 512 * q + c0 : 512 * q + c1], in_=res[:, c0:c1])
 
         for t in range(4):
             load(t)
@@ -194,7 +210,7 @@ def tile_regu_diff_kernel(tc, seg, W, out):
                 threshold(2 * s)
             if 0 <= s - LAG_SCALE < DUOS:
                 reciprocal(s - LAG_SCALE)
-                scale(s - LAG_SCALE)
+                scale_scalar(s - LAG_SCALE)
             if s == 2:
                 nc.vector.quantize_mx(
                     out=seg_codes[:].bitcast(FP8X4),
@@ -207,8 +223,15 @@ def tile_regu_diff_kernel(tc, seg, W, out):
                 turn(s - LAG_TURN)
             if 0 <= s - LAG_QUANT < DUOS:
                 quantise(s - LAG_QUANT)
+            if 0 <= s - LAG_SCALE < DUOS:
+                scale_vector(s - LAG_SCALE)
             if s < DUOS:
                 threshold(2 * s + 1)
                 pair_sums(s)
-            if 0 <= s - LAG_MX < DUOS and (s - LAG_MX) % 4 == 3:
-                store((s - LAG_MX) // 4)
+            done = s - LAG_MX
+            if 0 <= done < DUOS - 4 and done % 4 == 3:
+                store(done // 4, 0, 512)
+            if done == DUOS - 2:
+                store(done // 4, 0, 384)
+            if done == DUOS - 1:
+                store(done // 4, 384, 512)

@@ -60,8 +60,8 @@ def tile_regu_diff_kernel(tc, seg, W, out):
 
         part = const.tile([P, TILES], F32, name="part")
         recip = const.tile([P, TILES], F32, name="recip")
-        seg_sb = const.tile([P, N], BF16, name="seg_sb")
-        seg_g = const.tile([P, PASSES, P, 4], BF16, name="seg_g", align_bytes=64)
+        seg_a = const.tile([P, HALF], BF16, name="seg_a")
+        seg_b = const.tile([P, HALF], BF16, name="seg_b")
         seg_codes = const.tile([P, PASSES * P], U32, name="seg_codes", align_bytes=64)
         seg_scales = const.tile([P, PASSES * P], U8, name="seg_scales", align_bytes=64)
 
@@ -72,14 +72,16 @@ def tile_regu_diff_kernel(tc, seg, W, out):
         quants = {}
         accs = {}
 
-        def load(t):
-            win = win_pool.tile([P, HALF], BF16, name="win")
-            src = w2[t * ROWS : (t + 1) * ROWS, :].rearrange("m (g e x) -> e m g x", e=2, x=256)
+        def load_rows(dst, rows):
+            src = rows.rearrange("m (g e x) -> e m g x", e=2, x=256)
             for e in range(2):
                 nc.sync.dma_start(
-                    out=win[e:P:2, :].rearrange("q (g x) -> q g x", x=256), in_=src[e, :, :, :]
+                    out=dst[e:P:2, :].rearrange("q (g x) -> q g x", x=256), in_=src[e, :, :, :]
                 )
-            wins[t] = win
+
+        def load(t):
+            wins[t] = win_pool.tile([P, HALF], BF16, name="win")
+            load_rows(wins[t], w2[t * ROWS : (t + 1) * ROWS, :])
 
         def threshold(t):
             wt = wt_pool.tile([P, HALF], BF16, name="wt")
@@ -130,22 +132,22 @@ def tile_regu_diff_kernel(tc, seg, W, out):
                 out=ds[b][:, cut:], in0=wts[b][:, cut:], scalar1=recip[:, b : b + 1], scalar2=None, op0=ALU.mult
             )
 
-        def turn(s):
+        def turn(first, second):
             grouped = g_pool.tile([P, PASSES * 512], BF16, name="grouped", align_bytes=64)
-            groupeds[s] = grouped
             banks = []
             for bank in range(4):
                 xt = psum_t.tile([P, 1024], BF16, tag="xt", name="xt")
                 xv = xt[:].rearrange("p (g j m u e) -> p g j u m e", g=2, j=2, m=ROWS, u=2, e=2)
                 for gl in range(2):
                     g = 2 * bank + gl
-                    for j in range(2):
+                    for j, rows in enumerate((first, second)):
                         for u in range(2):
                             c0 = 256 * g + 128 * u
-                            nc.tensor.transpose(xv[:, gl, j, u, :, :], ds[2 * s + j][:, c0 : c0 + P], ident[:])
+                            nc.tensor.transpose(xv[:, gl, j, u, :, :], rows[:, c0 : c0 + P], ident[:])
                 banks.append(xt)
             for bank in range(4):
                 nc.scalar.copy(out=grouped[:, 1024 * bank : 1024 * (bank + 1)], in_=banks[bank][:])
+            return grouped
 
         def quantise(s):
             codes = q_pool.tile([P, PASSES * P], U32, name="codes", align_bytes=64)
@@ -185,22 +187,10 @@ def tile_regu_diff_kernel(tc, seg, W, out):
 
         for t in range(4):
             load(t)
-        nc.sync.dma_start(out=seg_sb[:], in_=seg_flat)
+        load_rows(seg_a, seg_flat[0:ROWS, :])
+        load_rows(seg_b, seg_flat[ROWS : 2 * ROWS, :])
         for t in range(4, 2 * AHEAD):
             load(t)
-        for half in range(PASSES // 2):
-            xs = psum_t.tile([P, 1024], BF16, tag="xt", name="xs")
-            xsv = xs[:].rearrange("p (a s d) -> p a s d", a=2, s=4)
-            for a in range(2):
-                g = 2 * half + a
-                for u in range(2):
-                    for e in range(2):
-                        k0 = 512 * g + 256 * e + 128 * u
-                        nc.tensor.transpose(xsv[:, a, 2 * u + e, :], seg_sb[:, k0 : k0 + P], ident[:])
-            nc.scalar.copy(
-                out=seg_g[:, 2 * half : 2 * half + 2, :, :],
-                in_=xs[:].rearrange("p (a s d) -> p a d s", a=2, s=4),
-            )
 
         for s in range(DUOS + LAG_MX + 1):
             if s + AHEAD < DUOS:
@@ -211,16 +201,16 @@ def tile_regu_diff_kernel(tc, seg, W, out):
             if 0 <= s - LAG_SCALE < DUOS:
                 reciprocal(s - LAG_SCALE)
                 scale_scalar(s - LAG_SCALE)
-            if s == 2:
+            if s == 1:
+                groupeds["seg"] = turn(seg_a, seg_b)
+            if s == 3:
                 nc.vector.quantize_mx(
-                    out=seg_codes[:].bitcast(FP8X4),
-                    scales=seg_scales[:],
-                    in_=seg_g[:].rearrange("p g d s -> p (g d s)"),
+                    out=seg_codes[:].bitcast(FP8X4), scales=seg_scales[:], in_=groupeds["seg"][:]
                 )
             if 0 <= s - LAG_MX < DUOS:
                 multiply(s - LAG_MX)
             if 0 <= s - LAG_TURN < DUOS:
-                turn(s - LAG_TURN)
+                groupeds[s - LAG_TURN] = turn(ds[2 * (s - LAG_TURN)], ds[2 * (s - LAG_TURN) + 1])
             if 0 <= s - LAG_QUANT < DUOS:
                 quantise(s - LAG_QUANT)
             if 0 <= s - LAG_SCALE < DUOS:

from contextlib import ExitStack

import concourse.mybir as mybir
from concourse.masks import make_identity

BF16 = mybir.dt.bfloat16
F32 = mybir.dt.float32
U32 = mybir.dt.uint32
U8 = mybir.dt.uint8
FP8X4 = mybir.dt.float8_e4m3fn_x4
ALU = mybir.AluOpType
ACT = mybir.ActivationFunctionType

P = 128
N = 4096
THRESH = 0.85
ROWS = 64
HALF = N // 2
TILES = N // ROWS
DUOS = TILES // 2
PASSES = 8
FLOPS = 2 * 128 * N * N

AHEAD = 3
LAG_SCALE = 1
LAG_TURN = 2
LAG_QUANT = 4
LAG_MX = 5
V_COLS = 768


def tile_regu_diff_kernel(tc, seg, W, out):
    nc = tc.nc
    seg_flat = seg.rearrange("b d r c -> (b d) (r c)")
    out_flat = out.rearrange("b d r c -> (b d) (r c)")
    w2 = W.rearrange("b m n -> (b m) n")

    with ExitStack() as ctx:
        ctx.enter_context(tc.manual_schedule())
        const = ctx.enter_context(tc.tile_pool(name="const", bufs=1))
        win_pool = ctx.enter_context(tc.tile_pool(name="win", bufs=2 * AHEAD + 2))
        wt_pool = ctx.enter_context(tc.tile_pool(name="wt", bufs=6))
        d_pool = ctx.enter_context(tc.tile_pool(name="d", bufs=6))
        g_pool = ctx.enter_context(tc.tile_pool(name="grouped", bufs=4))
        q_pool = ctx.enter_context(tc.tile_pool(name="quant", bufs=3))
        res_pool = ctx.enter_context(tc.tile_pool(name="res", bufs=2))
        psum_t = ctx.enter_context(tc.psum_pool(name="psum_t", bufs=5))
        psum_s = ctx.enter_context(tc.psum_pool(name="psum_s", bufs=1))
        psum_a = ctx.enter_context(tc.psum_pool(name="psum_a", bufs=2))

        ident = const.tile([P, P], BF16, name="ident")
        make_identity(nc, ident[:])
        ident32 = const.tile([P, P], F32, name="ident32")
        make_identity(nc, ident32[:])
        pair = const.tile([P, P], F32, name="pair")
        i3 = ident32[:].rearrange("p (j e) -> p j e", e=2)
        p3 = pair[:].rearrange("p (j e) -> p j e", e=2)
        for e in range(2):
            nc.vector.tensor_tensor(out=p3[:, :, e], in0=i3[:, :, 0], in1=i3[:, :, 1], op=ALU.add)

        part = const.tile([P, TILES], F32, name="part")
        recip = const.tile([P, TILES], F32, name="recip")
        seg_a = const.tile([P, HALF], BF16, name="seg_a")
        seg_b = const.tile([P, HALF], BF16, name="seg_b")
        seg_codes = const.tile([P, PASSES * P], U32, name="seg_codes", align_bytes=64)
        seg_scales = const.tile([P, PASSES * P], U8, name="seg_scales", align_bytes=64)

        wins = {}
        wts = {}
        ds = {}
        groupeds = {}
        quants = {}
        accs = {}

        def load_rows(dst, rows):
            src = rows.rearrange("m (g e x) -> e m g x", e=2, x=256)
            for e in range(2):
                nc.sync.dma_start(
                    out=dst[e:P:2, :].rearrange("q (g x) -> q g x", x=256), in_=src[e, :, :, :]
                )

        def load(t):
            wins[t] = win_pool.tile([P, HALF], BF16, name="win")
            load_rows(wins[t], w2[t * ROWS : (t + 1) * ROWS, :])

        def threshold(t):
            wt = wt_pool.tile([P, HALF], BF16, name="wt")
            nc.vector.scalar_tensor_tensor(
                out=wt[:],
                in0=wins[t][:],
                scalar=THRESH,
                in1=wins[t][:],
                op0=ALU.is_gt,
                op1=ALU.mult,
                accum_out=part[:, t : t + 1],
            )
            wts[t] = wt

        sums_of = {}

        def pair_sums(s):
            sums = psum_s.tile([P, 2], F32, name="sums")
            nc.tensor.matmul(out=sums[:], lhsT=pair[:], rhs=part[:, 2 * s : 2 * s + 2], start=True, stop=True)
            sums_of[s] = sums

        def reciprocal(s):
            nc.vector.reciprocal(out=recip[:, 2 * s : 2 * s + 2], in_=sums_of[s][:])

        def scale_scalar(s):
            a = 2 * s
            b = 2 * s + 1
            ds[a] = d_pool.tile([P, HALF], BF16, name="d")
            ds[b] = d_pool.tile([P, HALF], BF16, name="d")
            if s == DUOS - 1:
                return
            cut = HALF - V_COLS
            nc.scalar.activation(out=ds[a][:], in_=wts[a][:], func=ACT.Copy, scale=recip[:, a : a + 1])
            nc.scalar.activation(
                out=ds[b][:, :cut], in_=wts[b][:, :cut], func=ACT.Copy, scale=recip[:, b : b + 1]
            )

        def scale_vector(s):
            a = 2 * s
            b = 2 * s + 1
            cut = HALF - V_COLS
            if s == DUOS - 1:
                cut = 0
                nc.vector.tensor_scalar(
                    out=ds[a][:], in0=wts[a][:], scalar1=recip[:, a : a + 1], scalar2=None, op0=ALU.mult
                )
            nc.vector.tensor_scalar(
                out=ds[b][:, cut:], in0=wts[b][:, cut:], scalar1=recip[:, b : b + 1], scalar2=None, op0=ALU.mult
            )

        def turn(first, second):
            grouped = g_pool.tile([P, PASSES * 512], BF16, name="grouped", align_bytes=64)
            banks = []
            for bank in range(4):
                xt = psum_t.tile([P, 1024], BF16, tag="xt", name="xt")
                xv = xt[:].rearrange("p (g j m u e) -> p g j u m e", g=2, j=2, m=ROWS, u=2, e=2)
                for gl in range(2):
                    g = 2 * bank + gl
                    for j, rows in enumerate((first, second)):
                        for u in range(2):
                            c0 = 256 * g + 128 * u
                            nc.tensor.transpose(xv[:, gl, j, u, :, :], rows[:, c0 : c0 + P], ident[:])
                banks.append(xt)
            for bank in range(4):
                nc.scalar.copy(out=grouped[:, 1024 * bank : 1024 * (bank + 1)], in_=banks[bank][:])
            return grouped

        def quantise(s):
            codes = q_pool.tile([P, PASSES * P], U32, name="codes", align_bytes=64)
            scales = q_pool.tile([P, PASSES * P], U8, name="scales", align_bytes=64)
            pieces = 4 if s == DUOS - 1 else 1
            words = PASSES * P // pieces
            for i in range(pieces):
                nc.vector.quantize_mx(
                    out=codes[:, i * words : (i + 1) * words].bitcast(FP8X4),
                    scales=scales[:, i * words : (i + 1) * words],
                    in_=groupeds[s][:, 4 * i * words : 4 * (i + 1) * words],
                )
            quants[s] = (codes, scales)

        def multiply(s):
            if s % 4 == 0:
                accs[s // 4] = psum_a.tile([P, 512], F32, name="acc")
            acc = accs[s // 4]
            codes, scales = quants[s]
            c0 = (s % 4) * P
            for g in range(PASSES):
                cols = slice(g * P, (g + 1) * P)
                nc.tensor.matmul_mx(
                    out=acc[:, c0 : c0 + P],
                    lhsT=seg_codes[:, cols].bitcast(FP8X4),
                    lhsT_scale=seg_scales[:, cols],
                    rhs=codes[:, cols].bitcast(FP8X4),
                    rhs_scale=scales[:, cols],
                    start=(g == 0),
                    stop=(g == PASSES - 1),
                )

        def store(q, c0, c1):
            res = res_pool.tile([P, 512], F32, name="res")
            nc.scalar.copy(out=res[:, c0:c1], in_=accs[q][:, c0:c1])
            nc.sync.dma_start(out=out_flat[:, 512 * q + c0 : 512 * q + c1], in_=res[:, c0:c1])

        for t in range(4):
            load(t)
        load_rows(seg_a, seg_flat[0:ROWS, :])
        load_rows(seg_b, seg_flat[ROWS : 2 * ROWS, :])
        for t in range(4, 2 * AHEAD):
            load(t)

        for s in range(DUOS + LAG_MX + 1):
            if s + AHEAD < DUOS:
                load(2 * (s + AHEAD))
                load(2 * (s + AHEAD) + 1)
            if s < DUOS:
                threshold(2 * s)
            if 0 <= s - LAG_SCALE < DUOS:
                reciprocal(s - LAG_SCALE)
                scale_scalar(s - LAG_SCALE)
            if s == 1:
                groupeds["seg"] = turn(seg_a, seg_b)
            if s == 3:
                nc.vector.quantize_mx(
                    out=seg_codes[:].bitcast(FP8X4), scales=seg_scales[:], in_=groupeds["seg"][:]
                )
            if 0 <= s - LAG_MX < DUOS:
                multiply(s - LAG_MX)
            if 0 <= s - LAG_TURN < DUOS:
                groupeds[s - LAG_TURN] = turn(ds[2 * (s - LAG_TURN)], ds[2 * (s - LAG_TURN) + 1])
            if 0 <= s - LAG_QUANT < DUOS:
                quantise(s - LAG_QUANT)
            if 0 <= s - LAG_SCALE < DUOS:
                scale_vector(s - LAG_SCALE)
            if s < DUOS:
                threshold(2 * s + 1)
                pair_sums(s)
            done = s - LAG_MX
            if 0 <= done < DUOS - 4 and done % 4 == 3:
                store(done // 4, 0, 512)
            if done == DUOS - 2:
                store(done // 4, 0, 384)
            if done == DUOS - 1:
                store(done // 4, 384, 512)
